import numpy as np
import ml_dtypes


def mxq(x, axis, fmt="e4m3"):
    dtype, down = {"e4m3": (ml_dtypes.float8_e4m3fn, 7), "e5m2": (ml_dtypes.float8_e5m2, 14)}[fmt]
    v = np.moveaxis(np.asarray(x, np.float32).astype(ml_dtypes.bfloat16).astype(np.float64), axis, -1)
    blocks = v.reshape(v.shape[:-1] + (-1, 32))
    amax = np.abs(blocks).max(-1, keepdims=True)
    byte = np.maximum(np.where(amax > 0, np.frexp(amax)[1] - 1 + 127, 0) - down, 1)
    scale = np.exp2(byte - 127.0)
    codes = (blocks / scale).astype(np.float32).astype(dtype).astype(np.float64)
    return np.moveaxis((codes * scale).reshape(v.shape), -1, axis)


WIDE = False


def mx_kscale(k):
    if not WIDE:
        return np.ones(k)
    levels = np.array([10, -10, 5, -5, 0])
    a = np.random.permutation(np.resize(levels, k // 512 * 4)).reshape(k // 512, 4)
    idx = np.arange(k)
    return np.exp2(a[idx // 512, idx % 128 // 32])


BF16 = ml_dtypes.bfloat16


def bf(x):
    return np.asarray(x, np.float32).astype(BF16)


def f64(x):
    return np.asarray(x).astype(np.float64)


E2M1 = np.array([0.0, 0.5, 1.0, 1.5, 2.0, 3.0, 4.0, 6.0, -0.0, -0.5, -1.0, -1.5, -2.0, -3.0, -4.0, -6.0])


def pack_weight(w, fmt):
    k, n = w.shape
    w = f64(bf(w)).reshape(k // 32, 32, n)
    amax = np.abs(w).max(1)
    if fmt == "e4m3":
        byte = np.frexp(amax)[1] - 1 + 127 - 7
    else:
        mant, ex = np.frexp(amax / 6.0)
        byte = np.where(mant > 0.5, ex, ex - 1) + 127
    byte = np.clip(np.where(amax > 0, byte, 1), 1, 254)
    scaled = (w * np.exp2(127.0 - byte)[:, None, :]).reshape(k, n).astype(np.float32)
    by_word = np.ascontiguousarray(scaled.reshape(k // 512, 128, 4, n).transpose(0, 1, 3, 2))
    if fmt == "e4m3":
        words = by_word.astype(ml_dtypes.float8_e4m3fn).view(np.uint8)
    else:
        c = by_word.astype(ml_dtypes.float4_e2m1fn).view(np.uint8) & 0xF
        words = c[..., 0::2] | (c[..., 1::2] << 4)
    return np.ascontiguousarray(words), np.ascontiguousarray(byte.astype(np.uint8).reshape(k // 512, 16, n))


def unpack_weight(words, scales, fmt):
    g, p, n, _ = words.shape
    if fmt == "e4m3":
        vals = np.ascontiguousarray(words).view(ml_dtypes.float8_e4m3fn).astype(np.float64)
    else:
        nib = np.empty((g, p, n, 4), np.uint8)
        nib[..., 0::2] = words & 0xF
        nib[..., 1::2] = words >> 4
        vals = E2M1[nib]
    vals = vals * np.repeat(np.exp2(scales.astype(np.float64) - 127.0), 8, axis=1)[..., None]
    return vals.transpose(0, 1, 3, 2).reshape(g * 512, n)


B, D = 128, 3072
C = 8.0
FMT = "e4m3"


def sigmoid(v):
    return 1.0 / (1.0 + np.exp(-v))


def softplus(v):
    return np.logaddexp(v, 0.0)


def setup_inputs():
    s = mx_kscale(D)
    xt = bf(np.random.standard_normal((B, D)) * s)
    ht_minus_1 = bf(np.random.standard_normal((B, D)) * s)
    Wa = np.random.standard_normal((D, D)) / np.sqrt(D) / s[None, :]
    Wx = np.random.standard_normal((D, D)) / np.sqrt(D) / s[None, :]
    ba = bf(np.random.standard_normal((1, D)) * 0.1)
    bx = bf(np.random.standard_normal((1, D)) * 0.1)
    Lambda = bf(np.random.uniform(-3.0, -1.0, (1, D)))
    Wa_words, Wa_scales = pack_weight(np.ascontiguousarray(Wa.T), FMT)
    Wx_words, Wx_scales = pack_weight(np.ascontiguousarray(Wx.T), FMT)
    return {"xt": xt, "ht_minus_1": ht_minus_1, "Wa_words": Wa_words, "Wa_scales": Wa_scales, "Wx_words": Wx_words, "Wx_scales": Wx_scales, "ba": ba, "bx": bx, "Lambda": Lambda}


def reference(xt, ht_minus_1, Wa_words, Wa_scales, Wx_words, Wx_scales, ba, bx, Lambda):
    x = f64(xt)
    xq = mxq(x, 1, "e4m3")
    rt = sigmoid((xq @ unpack_weight(Wa_words, Wa_scales, FMT)) + f64(ba))
    it = sigmoid((xq @ unpack_weight(Wx_words, Wx_scales, FMT)) + f64(bx))
    log_at = -(C * softplus(f64(Lambda))) * rt
    at = np.exp(log_at)
    ht = at * f64(ht_minus_1) + np.sqrt(1.0 - at ** 2) * (it * x)
    return ht

@@ -1,0 +1,242 @@
+from contextlib import ExitStack
+
+import concourse.mybir as mybir
+from concourse.masks import make_identity
+
+FLOPS = 2 * 128 * 3072 * 3072 * 2
+
+F32 = mybir.dt.float32
+BF16 = mybir.dt.bfloat16
+I32 = mybir.dt.int32
+U32 = mybir.dt.uint32
+U8 = mybir.dt.uint8
+FP8X4 = mybir.dt.float8_e4m3fn_x4
+ACT = mybir.ActivationFunctionType
+ALU = mybir.AluOpType
+
+P = 128
+D = 3072
+G = 6
+NB = 512
+
+SCALES_ON_GPSIMD = False
+
+
+def tile_cell_w_kernel(
+    tc, xt, ht_minus_1, Wa_words, Wa_scales, Wx_words, Wx_scales, ba, bx, Lambda, out
+):
+    nc = tc.nc
+    with ExitStack() as ctx:
+        keep = ctx.enter_context(tc.tile_pool(name="keep", bufs=1))
+        wpool = ctx.enter_context(tc.tile_pool(name="wpool", bufs=1))
+        psum = ctx.enter_context(tc.psum_pool(name="psum", bufs=8))
+        ctx.enter_context(tc.manual_schedule())
+
+        x_sb = keep.tile([P, D], BF16, name="x_sb")
+        h_sb = keep.tile([P, D], BF16, name="h_sb")
+        grouped = keep.tile([P, D], BF16, name="grouped", align_bytes=64)
+        xcodes = keep.tile([P, G * P], U32, name="xcodes", align_bytes=64)
+        xsc = keep.tile([P, G * P], U8, name="xsc", align_bytes=64)
+        planes = keep.tile([P, 3, D], U8, name="planes", align_bytes=64)
+        ident_f = keep.tile([P, P], F32, name="ident_f")
+        ident_b = keep.tile([P, P], BF16, name="ident_b")
+        zrows = keep.tile([P, NB], BF16, name="zrows")
+        lrows = keep.tile([P, P], BF16, name="lrows")
+        warm = keep.tile([P, 1], F32, name="warm")
+        warm2 = keep.tile([P, 1], F32, name="warm2")
+        r24 = keep.tile([P, 24], F32, name="r24")
+        nv24 = keep.tile([P, 24], F32, name="nv24")
+        spv = keep.tile([P, 24], F32, name="spv")
+        ba_bc = keep.tile([P, D], BF16, name="ba_bc")
+        bx_bc = keep.tile([P, D], BF16, name="bx_bc")
+        A = keep.tile([P, D], F32, name="A")
+        B = keep.tile([P, D], F32, name="B")
+        S = keep.tile([P, D], F32, name="S")
+
+        def bank(shape, dtype, name):
+            return psum.tile(shape, dtype, tag="bank", name=name)
+
+        def load_words(words, g, c0, c1, slot, name):
+            t = wpool.tile([P, c1 - c0], U32, tag=slot, name=name, align_bytes=64)
+            src = words[g].rearrange("p n t -> p (n t)")[:, 4 * c0 : 4 * c1]
+            nc.sync.dma_start(out=t[:].bitcast(I32), in_=src.bitcast(I32))
+            return t
+
+        def table(func):
+            nc.scalar.activation(out=warm2[:], in_=warm[:], func=func)
+
+        nc.sync.dma_start(out=x_sb[:], in_=xt)
+        nc.vector.memset(lrows[:], 0.0)
+        nc.vector.memset(zrows[:], 0.0)
+        nc.vector.memset(warm[:], 1.0)
+        for T in range(3):
+            nc.vector.memset(planes[:, T, :].bitcast(I32), 0)
+        nc.scalar.dma_start(out=lrows[0:24, :], in_=Lambda.rearrange("o (r c) -> (o r) c", c=P))
+        nc.scalar.dma_start(out=zrows[0:6, :], in_=ba.rearrange("o (r c) -> (o r) c", c=NB))
+        nc.scalar.dma_start(out=zrows[6:12, :], in_=bx.rearrange("o (r c) -> (o r) c", c=NB))
+        table(ACT.Exp)
+        make_identity(nc, ident_b[:])
+        make_identity(nc, ident_f[:])
+
+        plane_loads = [
+            (0, 0, 16, Wa_scales, 0, 4),
+            (1, 0, 8, Wa_scales, 4, 6),
+            (1, 8, 8, Wx_scales, 4, 6),
+            (2, 0, 16, Wx_scales, 0, 4),
+        ]
+        for T, p0, n_p, src, g0, g1 in plane_loads:
+            for Q in range(4):
+                dst = planes[32 * Q + p0 : 32 * Q + p0 + n_p, T, :]
+                rows = src[g0:g1, 4 * Q : 4 * Q + 4, :]
+                if SCALES_ON_GPSIMD:
+                    nc.gpsimd.dma_start(out=dst.bitcast(F32), in_=rows.bitcast(F32))
+                else:
+                    nc.sync.dma_start(out=dst.bitcast(I32), in_=rows.bitcast(I32))
+
+        def plane_of(is_a, g):
+            if g < 4:
+                return (0 if is_a else 2), 4 * g
+            return 1, (0 if is_a else 8) + 4 * (g - 4)
+
+        wa1 = [load_words(Wa_words, g, 0, 1536, "ws%d" % g, "wa1_%d" % g) for g in range(G)]
+        nc.sync.dma_start(out=h_sb[:], in_=ht_minus_1)
+        wa2 = [load_words(Wa_words, g, 1536, 3072, "ws%d" % (6 + g), "wa2_%d" % g) for g in range(G)]
+        wx1 = [load_words(Wx_words, g, 0, 1536, "ws%d" % (12 + g), "wx1_%d" % g) for g in range(G)]
+
+        lt_ps = bank([P, P], BF16, "lt_ps")
+        nc.tensor.transpose(out=lt_ps[:], in_=lrows[:], identity=ident_b[:])
+        nc.vector.tensor_scalar_max(out=r24[:], in0=lt_ps[:, 0:24], scalar1=0.0)
+        nc.vector.scalar_tensor_tensor(
+            out=nv24[:], in0=lt_ps[:, 0:24], scalar=0.0, in1=r24[:], op0=ALU.min, op1=ALU.subtract
+        )
+        nc.scalar.activation(out=nv24[:], in_=nv24[:], func=ACT.Exp)
+        nc.scalar.activation(out=nv24[:], in_=nv24[:], func=ACT.Ln, bias=1.0)
+
+        xw = x_sb[:].bitcast(F32)
+        gw = grouped[:].bitcast(F32).rearrange("p (g b u) -> p g b u", g=G, b=P, u=2)
+        for j in range(3):
+            t = bank([P, 4, P], F32, "xt_ps%d" % j)
+            for i in range(4):
+                g, u = 2 * j + i // 2, i % 2
+                nc.tensor.transpose(
+                    out=t[:, i, :], in_=xw[:, 256 * g + u : 256 * (g + 1) : 2], identity=ident_f[:]
+                )
+            nc.vector.tensor_copy(
+                out=gw[:, 2 * j : 2 * j + 2], in_=t[:].rearrange("p (g u) b -> p g b u", u=2)
+            )
+        nc.vector.quantize_mx(
+            out=xcodes[:, 0:256].bitcast(FP8X4), scales=xsc[:, 0:256], in_=grouped[:, 0:1024]
+        )
+        nc.vector.quantize_mx(
+            out=xcodes[:, 256:768].bitcast(FP8X4), scales=xsc[:, 256:768], in_=grouped[:, 1024:3072]
+        )
+        nc.vector.tensor_tensor(out=spv[:], in0=r24[:], in1=nv24[:], op=ALU.add)
+
+        def spread_bias(row0, dst, name):
+            for i in range(3):
+                t = bank([P, 2 * NB], BF16, "%s%d" % (name, i))
+                for half in range(2):
+                    r = row0 + 2 * i + half
+                    nc.tensor.matmul(
+                        out=t[:, NB * half : NB * (half + 1)],
+                        lhsT=ident_b[:, r : r + 1].to_broadcast([P, P]),
+                        rhs=zrows[:],
+                        start=True,
+                        stop=True,
+                    )
+                nc.scalar.copy(out=dst[:, 2 * NB * i : 2 * NB * (i + 1)], in_=t[:])
+
+        spread_bias(0, ba_bc, "ba_ps")
+        for jb in range(6):
+            t = bank([P, 4, P], F32, "sp_ps%d" % jb)
+            for i in range(4):
+                j = 4 * jb + i
+                nc.tensor.transpose(
+                    out=t[:, i, :], in_=spv[:, j : j + 1].to_broadcast([P, P]), identity=ident_f[:]
+                )
+            dst = S[:, NB * jb : NB * (jb + 1)]
+            if jb % 2 == 0:
+                nc.vector.tensor_copy(out=dst, in_=t[:].rearrange("p i c -> p (i c)"))
+            else:
+                nc.scalar.copy(out=dst, in_=t[:].rearrange("p i c -> p (i c)"))
+        spread_bias(6, bx_bc, "bx_ps")
+        table(ACT.Tanh)
+
+        def mx_range(is_a, wt, c0, n_banks, name):
+            acc = [bank([P, NB], F32, "%s%d" % (name, b)) for b in range(n_banks)]
+            for g in range(G):
+                T, k = plane_of(is_a, g)
+                for b in range(n_banks):
+                    nc.tensor.matmul_mx(
+                        out=acc[b][:],
+                        lhsT=xcodes[:, P * g : P * (g + 1)].bitcast(FP8X4),
+                        lhsT_scale=xsc[:, P * g : P * (g + 1)],
+                        rhs=wt[g][:, NB * b : NB * (b + 1)].bitcast(FP8X4),
+                        rhs_scale=planes[k:P, T, c0 + NB * b : c0 + NB * (b + 1)],
+                        start=(g == 0),
+                        stop=(g == G - 1),
+                    )
+            return acc
+
+        def phase_a(c0, acc):
+            cols = [slice(c0 + NB * b, c0 + NB * (b + 1)) for b in range(len(acc))]
+            for b, cs in enumerate(cols):
+                nc.vector.tensor_tensor(out=A[:, cs], in0=acc[b][:], in1=ba_bc[:, cs], op=ALU.add)
+            for cs in cols:
+                nc.scalar.activation(out=A[:, cs], in_=A[:, cs], func=ACT.Tanh, scale=0.5)
+            for cs in cols:
+                nc.vector.scalar_tensor_tensor(
+                    out=A[:, cs], in0=A[:, cs], scalar=1.0, in1=S[:, cs], op0=ALU.add, op1=ALU.mult
+                )
+            for cs in cols:
+                nc.scalar.activation(out=B[:, cs], in_=A[:, cs], func=ACT.Exp, scale=-4.0)
+            table(ACT.Sqrt)
+            for cs in cols:
+                nc.vector.scalar_tensor_tensor(
+                    out=A[:, cs], in0=B[:, cs], scalar=-0.25, in1=B[:, cs], op0=ALU.mult, op1=ALU.mult
+                )
+                nc.vector.tensor_tensor(out=B[:, cs], in0=B[:, cs], in1=h_sb[:, cs], op=ALU.mult)
+            for cs in cols:
+                nc.scalar.activation(out=A[:, cs], in_=A[:, cs], func=ACT.Sqrt, bias=0.25)
+            table(ACT.Tanh)
+            for cs in cols:
+                nc.vector.scalar_tensor_tensor(
+                    out=A[:, cs], in0=A[:, cs], scalar=0.0, in1=x_sb[:, cs], op0=ALU.max, op1=ALU.mult
+                )
+
+        def phase_b(pieces, stores):
+            for src, cs in pieces:
+                nc.vector.tensor_tensor(out=S[:, cs], in0=src, in1=bx_bc[:, cs], op=ALU.add)
+            for src, cs in pieces:
+                nc.scalar.activation(out=S[:, cs], in_=S[:, cs], func=ACT.Tanh, scale=0.5)
+            for i, (src, cs) in enumerate(pieces):
+                nc.vector.scalar_tensor_tensor(
+                    out=S[:, cs], in0=S[:, cs], scalar=1.0, in1=A[:, cs], op0=ALU.add, op1=ALU.mult
+                )
+                nc.vector.tensor_tensor(out=B[:, cs], in0=B[:, cs], in1=S[:, cs], op=ALU.add)
+                if stores is None:
+                    nc.sync.dma_start(out=out[:, cs], in_=B[:, cs])
+            if stores is not None:
+                nc.sync.dma_start(out=out[:, stores], in_=B[:, stores])
+
+        acc_a1 = mx_range(True, wa1, 0, 3, "a1_")
+        wx2 = [load_words(Wx_words, g, 1536, 2560, "ws%d" % g, "wx2_%d" % g) for g in range(G)]
+        wx3 = [load_words(Wx_words, g, 2560, 3072, "wt%d" % g, "wx3_%d" % g) for g in range(G)]
+        phase_a(0, acc_a1)
+        acc_a2 = mx_range(True, wa2, 1536, 3, "a2_")
+        phase_a(1536, acc_a2)
+
+        acc_b1 = mx_range(False, wx1, 0, 3, "b1_")
+        phase_b(
+            [(acc_b1[b][:], slice(NB * b, NB * (b + 1))) for b in range(3)], slice(0, 1536)
+        )
+        acc_b2 = mx_range(False, wx2, 1536, 2, "b2_")
+        phase_b(
+            [(acc_b2[b][:], slice(1536 + NB * b, 1536 + NB * (b + 1))) for b in range(2)],
+            slice(1536, 2560),
+        )
+        acc_b3 = mx_range(False, wx3, 2560, 1, "b3_")
+        phase_b(
+            [(acc_b3[0][:, 256 * i : 256 * (i + 1)], slice(2560 + 256 * i, 2560 + 256 * (i + 1))) for i in range(2)],
+            None,
+        )

@@ -19,7 +19,7 @@ D = 3072
 G = 6
 NB = 512
 
-SCALES_ON_GPSIMD = False
+SCALES_ON_GPSIMD = True
 
 
 def tile_cell_w_kernel(

@@ -19,8 +19,6 @@ D = 3072
 G = 6
 NB = 512
 
-SCALES_ON_GPSIMD = True
-
 
 def tile_cell_w_kernel(
     tc, xt, ht_minus_1, Wa_words, Wa_scales, Wx_words, Wx_scales, ba, bx, Lambda, out
@@ -66,17 +64,20 @@ def tile_cell_w_kernel(
             nc.scalar.activation(out=warm2[:], in_=warm[:], func=func)
 
         nc.sync.dma_start(out=x_sb[:], in_=xt)
+        nc.vector.memset(planes[:, 0, :].bitcast(I32), 0)
+        nc.vector.memset(ident_b[:], 0.0)
+        nc.vector.memset(ident_f[:], 0.0)
         nc.vector.memset(lrows[:], 0.0)
         nc.vector.memset(zrows[:], 0.0)
         nc.vector.memset(warm[:], 1.0)
-        for T in range(3):
-            nc.vector.memset(planes[:, T, :].bitcast(I32), 0)
+        nc.vector.memset(planes[:, 1, :].bitcast(I32), 0)
+        nc.vector.memset(planes[:, 2, :].bitcast(I32), 0)
         nc.scalar.dma_start(out=lrows[0:24, :], in_=Lambda.rearrange("o (r c) -> (o r) c", c=P))
         nc.scalar.dma_start(out=zrows[0:6, :], in_=ba.rearrange("o (r c) -> (o r) c", c=NB))
         nc.scalar.dma_start(out=zrows[6:12, :], in_=bx.rearrange("o (r c) -> (o r) c", c=NB))
         table(ACT.Exp)
-        make_identity(nc, ident_b[:])
-        make_identity(nc, ident_f[:])
+        make_identity(nc, ident_b[:], nomemset=True)
+        make_identity(nc, ident_f[:], nomemset=True)
 
         plane_loads = [
             (0, 0, 16, Wa_scales, 0, 4),
@@ -88,10 +89,7 @@ def tile_cell_w_kernel(
             for Q in range(4):
                 dst = planes[32 * Q + p0 : 32 * Q + p0 + n_p, T, :]
                 rows = src[g0:g1, 4 * Q : 4 * Q + 4, :]
-                if SCALES_ON_GPSIMD:
-                    nc.gpsimd.dma_start(out=dst.bitcast(F32), in_=rows.bitcast(F32))
-                else:
-                    nc.sync.dma_start(out=dst.bitcast(I32), in_=rows.bitcast(I32))
+                nc.gpsimd.dma_start(out=dst.bitcast(F32), in_=rows.bitcast(F32))
 
         def plane_of(is_a, g):
             if g < 4:
@@ -111,25 +109,6 @@ def tile_cell_w_kernel(
         )
         nc.scalar.activation(out=nv24[:], in_=nv24[:], func=ACT.Exp)
         nc.scalar.activation(out=nv24[:], in_=nv24[:], func=ACT.Ln, bias=1.0)
-
-        xw = x_sb[:].bitcast(F32)
-        gw = grouped[:].bitcast(F32).rearrange("p (g b u) -> p g b u", g=G, b=P, u=2)
-        for j in range(3):
-            t = bank([P, 4, P], F32, "xt_ps%d" % j)
-            for i in range(4):
-                g, u = 2 * j + i // 2, i % 2
-                nc.tensor.transpose(
-                    out=t[:, i, :], in_=xw[:, 256 * g + u : 256 * (g + 1) : 2], identity=ident_f[:]
-                )
-            nc.vector.tensor_copy(
-                out=gw[:, 2 * j : 2 * j + 2], in_=t[:].rearrange("p (g u) b -> p g b u", u=2)
-            )
-        nc.vector.quantize_mx(
-            out=xcodes[:, 0:256].bitcast(FP8X4), scales=xsc[:, 0:256], in_=grouped[:, 0:1024]
-        )
-        nc.vector.quantize_mx(
-            out=xcodes[:, 256:768].bitcast(FP8X4), scales=xsc[:, 256:768], in_=grouped[:, 1024:3072]
-        )
         nc.vector.tensor_tensor(out=spv[:], in0=r24[:], in1=nv24[:], op=ALU.add)
 
         def spread_bias(row0, dst, name):
@@ -146,8 +125,7 @@ def tile_cell_w_kernel(
                     )
                 nc.scalar.copy(out=dst[:, 2 * NB * i : 2 * NB * (i + 1)], in_=t[:])
 
-        spread_bias(0, ba_bc, "ba_ps")
-        for jb in range(6):
+        def spread_softplus(jb):
             t = bank([P, 4, P], F32, "sp_ps%d" % jb)
             for i in range(4):
                 j = 4 * jb + i
@@ -159,14 +137,45 @@ def tile_cell_w_kernel(
                 nc.vector.tensor_copy(out=dst, in_=t[:].rearrange("p i c -> p (i c)"))
             else:
                 nc.scalar.copy(out=dst, in_=t[:].rearrange("p i c -> p (i c)"))
-        spread_bias(6, bx_bc, "bx_ps")
-        table(ACT.Tanh)
 
-        def mx_range(is_a, wt, c0, n_banks, name):
-            acc = [bank([P, NB], F32, "%s%d" % (name, b)) for b in range(n_banks)]
-            for g in range(G):
+        spread_bias(0, ba_bc, "ba_ps")
+
+        xw = x_sb[:].bitcast(F32)
+        gw = grouped[:].bitcast(F32).rearrange("p (g b u) -> p g b u", g=G, b=P, u=2)
+        xt_ps = []
+        for j in range(3):
+            t = bank([P, 4, P], F32, "xt_ps%d" % j)
+            for i in range(4):
+                g, u = 2 * j + i // 2, i % 2
+                nc.tensor.transpose(
+                    out=t[:, i, :], in_=xw[:, 256 * g + u : 256 * (g + 1) : 2], identity=ident_f[:]
+                )
+            xt_ps.append(t)
+
+        def x_out(eng_copy, j):
+            eng_copy(out=gw[:, 2 * j : 2 * j + 2], in_=xt_ps[j][:].rearrange("p (g u) b -> p g b u", u=2))
+
+        def x_quant(j):
+            nc.vector.quantize_mx(
+                out=xcodes[:, 256 * j : 256 * (j + 1)].bitcast(FP8X4),
+                scales=xsc[:, 256 * j : 256 * (j + 1)],
+                in_=grouped[:, 1024 * j : 1024 * (j + 1)],
+            )
+
+        x_out(nc.vector.tensor_copy, 0)
+        x_out(nc.scalar.copy, 1)
+        x_out(nc.vector.tensor_copy, 2)
+        x_quant(0)
+        x_quant(1)
+        x_quant(2)
+
+        def mx_banks(n_banks, name):
+            return [bank([P, NB], F32, "%s%d" % (name, b)) for b in range(n_banks)]
+
+        def mx_passes(is_a, wt, c0, acc, groups):
+            for g in groups:
                 T, k = plane_of(is_a, g)
-                for b in range(n_banks):
+                for b in range(len(acc)):
                     nc.tensor.matmul_mx(
                         out=acc[b][:],
                         lhsT=xcodes[:, P * g : P * (g + 1)].bitcast(FP8X4),
@@ -176,10 +185,18 @@ def tile_cell_w_kernel(
                         start=(g == 0),
                         stop=(g == G - 1),
                     )
-            return acc
 
         def phase_a(c0, acc):
             cols = [slice(c0 + NB * b, c0 + NB * (b + 1)) for b in range(len(acc))]
+
+            def square(cs):
+                nc.vector.scalar_tensor_tensor(
+                    out=A[:, cs], in0=B[:, cs], scalar=-0.25, in1=B[:, cs], op0=ALU.mult, op1=ALU.mult
+                )
+
+            def times_h(cs):
+                nc.vector.tensor_tensor(out=B[:, cs], in0=B[:, cs], in1=h_sb[:, cs], op=ALU.mult)
+
             for b, cs in enumerate(cols):
                 nc.vector.tensor_tensor(out=A[:, cs], in0=acc[b][:], in1=ba_bc[:, cs], op=ALU.add)
             for cs in cols:
@@ -191,11 +208,12 @@ def tile_cell_w_kernel(
             for cs in cols:
                 nc.scalar.activation(out=B[:, cs], in_=A[:, cs], func=ACT.Exp, scale=-4.0)
             table(ACT.Sqrt)
-            for cs in cols:
-                nc.vector.scalar_tensor_tensor(
-                    out=A[:, cs], in0=B[:, cs], scalar=-0.25, in1=B[:, cs], op0=ALU.mult, op1=ALU.mult
-                )
-                nc.vector.tensor_tensor(out=B[:, cs], in0=B[:, cs], in1=h_sb[:, cs], op=ALU.mult)
+            square(cols[0])
+            square(cols[1])
+            times_h(cols[0])
+            square(cols[2])
+            times_h(cols[1])
+            times_h(cols[2])
             for cs in cols:
                 nc.scalar.activation(out=A[:, cs], in_=A[:, cs], func=ACT.Sqrt, bias=0.25)
             table(ACT.Tanh)
@@ -205,37 +223,57 @@ def tile_cell_w_kernel(
                 )
 
         def phase_b(pieces, stores):
+            def gate(cs):
+                nc.vector.scalar_tensor_tensor(
+                    out=S[:, cs], in0=S[:, cs], scalar=1.0, in1=A[:, cs], op0=ALU.add, op1=ALU.mult
+                )
+
+            def total(cs):
+                nc.vector.tensor_tensor(out=B[:, cs], in0=B[:, cs], in1=S[:, cs], op=ALU.add)
+                if stores is None:
+                    nc.sync.dma_start(out=out[:, cs], in_=B[:, cs])
+
             for src, cs in pieces:
                 nc.vector.tensor_tensor(out=S[:, cs], in0=src, in1=bx_bc[:, cs], op=ALU.add)
             for src, cs in pieces:
                 nc.scalar.activation(out=S[:, cs], in_=S[:, cs], func=ACT.Tanh, scale=0.5)
-            for i, (src, cs) in enumerate(pieces):
-                nc.vector.scalar_tensor_tensor(
-                    out=S[:, cs], in0=S[:, cs], scalar=1.0, in1=A[:, cs], op0=ALU.add, op1=ALU.mult
-                )
-                nc.vector.tensor_tensor(out=B[:, cs], in0=B[:, cs], in1=S[:, cs], op=ALU.add)
-                if stores is None:
-                    nc.sync.dma_start(out=out[:, cs], in_=B[:, cs])
+            gate(pieces[0][1])
+            for i in range(1, len(pieces)):
+                gate(pieces[i][1])
+                total(pieces[i - 1][1])
+            total(pieces[-1][1])
             if stores is not None:
                 nc.sync.dma_start(out=out[:, stores], in_=B[:, stores])
 
-        acc_a1 = mx_range(True, wa1, 0, 3, "a1_")
+        for jb in range(3):
+            spread_softplus(jb)
+        table(ACT.Tanh)
+        acc_a1 = mx_banks(3, "a1_")
+        mx_passes(True, wa1, 0, acc_a1, range(0, 4))
+        for jb in range(3, 6):
+            spread_softplus(jb)
+        mx_passes(True, wa1, 0, acc_a1, range(4, 6))
         wx2 = [load_words(Wx_words, g, 1536, 2560, "ws%d" % g, "wx2_%d" % g) for g in range(G)]
         wx3 = [load_words(Wx_words, g, 2560, 3072, "wt%d" % g, "wx3_%d" % g) for g in range(G)]
         phase_a(0, acc_a1)
-        acc_a2 = mx_range(True, wa2, 1536, 3, "a2_")
+        spread_bias(6, bx_bc, "bx_ps")
+        acc_a2 = mx_banks(3, "a2_")
+        mx_passes(True, wa2, 1536, acc_a2, range(G))
         phase_a(1536, acc_a2)
 
-        acc_b1 = mx_range(False, wx1, 0, 3, "b1_")
+        acc_b1 = mx_banks(3, "b1_")
+        mx_passes(False, wx1, 0, acc_b1, range(G))
         phase_b(
             [(acc_b1[b][:], slice(NB * b, NB * (b + 1))) for b in range(3)], slice(0, 1536)
         )
-        acc_b2 = mx_range(False, wx2, 1536, 2, "b2_")
+        acc_b2 = mx_banks(2, "b2_")
+        mx_passes(False, wx2, 1536, acc_b2, range(G))
         phase_b(
             [(acc_b2[b][:], slice(1536 + NB * b, 1536 + NB * (b + 1))) for b in range(2)],
             slice(1536, 2560),
         )
-        acc_b3 = mx_range(False, wx3, 2560, 1, "b3_")
+        acc_b3 = mx_banks(1, "b3_")
+        mx_passes(False, wx3, 2560, acc_b3, range(G))
         phase_b(
             [(acc_b3[0][:, 256 * i : 256 * (i + 1)], slice(2560 + 256 * i, 2560 + 256 * (i + 1))) for i in range(2)],
             None,

@@ -82,8 +82,8 @@ def tile_cell_w_kernel(
         plane_loads = [
             (0, 0, 16, Wa_scales, 0, 4),
             (1, 0, 8, Wa_scales, 4, 6),
-            (1, 8, 8, Wx_scales, 4, 6),
             (2, 0, 16, Wx_scales, 0, 4),
+            (1, 8, 8, Wx_scales, 4, 6),
         ]
         for T, p0, n_p, src, g0, g1 in plane_loads:
             for Q in range(4):
@@ -222,28 +222,22 @@ def tile_cell_w_kernel(
                     out=A[:, cs], in0=A[:, cs], scalar=0.0, in1=x_sb[:, cs], op0=ALU.max, op1=ALU.mult
                 )
 
-        def phase_b(pieces, stores):
-            def gate(cs):
-                nc.vector.scalar_tensor_tensor(
-                    out=S[:, cs], in0=S[:, cs], scalar=1.0, in1=A[:, cs], op0=ALU.add, op1=ALU.mult
-                )
+        def b_bias(src, cs):
+            nc.vector.tensor_tensor(out=S[:, cs], in0=src, in1=bx_bc[:, cs], op=ALU.add)
 
-            def total(cs):
-                nc.vector.tensor_tensor(out=B[:, cs], in0=B[:, cs], in1=S[:, cs], op=ALU.add)
-                if stores is None:
-                    nc.sync.dma_start(out=out[:, cs], in_=B[:, cs])
+        def b_tanh(cs):
+            nc.scalar.activation(out=S[:, cs], in_=S[:, cs], func=ACT.Tanh, scale=0.5)
 
-            for src, cs in pieces:
-                nc.vector.tensor_tensor(out=S[:, cs], in0=src, in1=bx_bc[:, cs], op=ALU.add)
-            for src, cs in pieces:
-                nc.scalar.activation(out=S[:, cs], in_=S[:, cs], func=ACT.Tanh, scale=0.5)
-            gate(pieces[0][1])
-            for i in range(1, len(pieces)):
-                gate(pieces[i][1])
-                total(pieces[i - 1][1])
-            total(pieces[-1][1])
-            if stores is not None:
-                nc.sync.dma_start(out=out[:, stores], in_=B[:, stores])
+        def b_gate(cs):
+            nc.vector.scalar_tensor_tensor(
+                out=S[:, cs], in0=S[:, cs], scalar=1.0, in1=A[:, cs], op0=ALU.add, op1=ALU.mult
+            )
+
+        def b_total(cs):
+            nc.vector.tensor_tensor(out=B[:, cs], in0=B[:, cs], in1=S[:, cs], op=ALU.add)
+
+        def store(cs):
+            nc.sync.dma_start(out=out[:, cs], in_=B[:, cs])
 
         for jb in range(3):
             spread_softplus(jb)
@@ -263,18 +257,44 @@ def tile_cell_w_kernel(
 
         acc_b1 = mx_banks(3, "b1_")
         mx_passes(False, wx1, 0, acc_b1, range(G))
-        phase_b(
-            [(acc_b1[b][:], slice(NB * b, NB * (b + 1))) for b in range(3)], slice(0, 1536)
-        )
+        c1 = [slice(NB * b, NB * (b + 1)) for b in range(3)]
+        for b in range(3):
+            b_bias(acc_b1[b][:], c1[b])
+        for b in range(3):
+            b_tanh(c1[b])
+        for b in range(3):
+            b_gate(c1[b])
+        for b in range(3):
+            b_total(c1[b])
+        store(slice(0, 1536))
+
         acc_b2 = mx_banks(2, "b2_")
         mx_passes(False, wx2, 1536, acc_b2, range(G))
-        phase_b(
-            [(acc_b2[b][:], slice(1536 + NB * b, 1536 + NB * (b + 1))) for b in range(2)],
-            slice(1536, 2560),
-        )
+        c2 = [slice(1536, 1792), slice(1792, 2048), slice(2048, 2560)]
+        b_bias(acc_b2[0][:, 0:256], c2[0])
+        b_bias(acc_b2[0][:, 256:512], c2[1])
+        b_bias(acc_b2[1][:], c2[2])
+        for cs in c2:
+            b_tanh(cs)
+        b_gate(c2[0])
+        b_gate(c2[1])
+        b_total(c2[0])
+        b_total(c2[1])
+        store(slice(1536, 2048))
+        b_gate(c2[2])
+
         acc_b3 = mx_banks(1, "b3_")
         mx_passes(False, wx3, 2560, acc_b3, range(G))
-        phase_b(
-            [(acc_b3[0][:, 256 * i : 256 * (i + 1)], slice(2560 + 256 * i, 2560 + 256 * (i + 1))) for i in range(2)],
-            None,
-        )
+        c3 = [slice(2560, 2816), slice(2816, 3072)]
+        b_bias(acc_b3[0][:, 0:256], c3[0])
+        b_bias(acc_b3[0][:, 256:512], c3[1])
+        b_tanh(c3[0])
+        b_tanh(c3[1])
+        b_total(c2[2])
+        store(c2[2])
+        b_gate(c3[0])
+        b_gate(c3[1])
+        b_total(c3[0])
+        store(c3[0])
+        b_total(c3[1])
+        store(c3[1])

@@ -18,6 +18,7 @@ P = 128
 D = 3072
 G = 6
 NB = 512
+GROUPS_PER_DMA = (3, 2, 1)
 
 
 def tile_cell_w_kernel(
@@ -54,11 +55,19 @@ def tile_cell_w_kernel(
         def bank(shape, dtype, name):
             return psum.tile(shape, dtype, tag="bank", name=name)
 
-        def load_words(words, g, c0, c1, slot, name):
-            t = wpool.tile([P, c1 - c0], U32, tag=slot, name=name, align_bytes=64)
-            src = words[g].rearrange("p n t -> p (n t)")[:, 4 * c0 : 4 * c1]
-            nc.sync.dma_start(out=t[:].bitcast(I32), in_=src.bitcast(I32))
-            return t
+        def load_range(words, c0, c1, slot, name):
+            views = []
+            g0 = 0
+            for i, n_g in enumerate(GROUPS_PER_DMA):
+                t = wpool.tile(
+                    [P, n_g, c1 - c0], U32, tag="%s_%d" % (slot, i), name="%s_%d" % (name, i), align_bytes=64
+                )
+                src = words[g0 : g0 + n_g].rearrange("g p n t -> p g (n t)")[:, :, 4 * c0 : 4 * c1]
+                nc.sync.dma_start(out=t[:].bitcast(I32), in_=src.bitcast(I32))
+                for j in range(n_g):
+                    views.append(t[:, j, :])
+                g0 += n_g
+            return views
 
         def table(func):
             nc.scalar.activation(out=warm2[:], in_=warm[:], func=func)
@@ -82,8 +91,8 @@ def tile_cell_w_kernel(
         plane_loads = [
             (0, 0, 16, Wa_scales, 0, 4),
             (1, 0, 8, Wa_scales, 4, 6),
-            (2, 0, 16, Wx_scales, 0, 4),
             (1, 8, 8, Wx_scales, 4, 6),
+            (2, 0, 16, Wx_scales, 0, 4),
         ]
         for T, p0, n_p, src, g0, g1 in plane_loads:
             for Q in range(4):
@@ -96,10 +105,10 @@ def tile_cell_w_kernel(
                 return (0 if is_a else 2), 4 * g
             return 1, (0 if is_a else 8) + 4 * (g - 4)
 
-        wa1 = [load_words(Wa_words, g, 0, 1536, "ws%d" % g, "wa1_%d" % g) for g in range(G)]
+        wa1 = load_range(Wa_words, 0, 1536, "s0", "wa1")
         nc.sync.dma_start(out=h_sb[:], in_=ht_minus_1)
-        wa2 = [load_words(Wa_words, g, 1536, 3072, "ws%d" % (6 + g), "wa2_%d" % g) for g in range(G)]
-        wx1 = [load_words(Wx_words, g, 0, 1536, "ws%d" % (12 + g), "wx1_%d" % g) for g in range(G)]
+        wa2 = load_range(Wa_words, 1536, 3072, "s1", "wa2")
+        wx1 = load_range(Wx_words, 0, 1536, "s2", "wx1")
 
         lt_ps = bank([P, P], BF16, "lt_ps")
         nc.tensor.transpose(out=lt_ps[:], in_=lrows[:], identity=ident_b[:])
@@ -222,22 +231,28 @@ def tile_cell_w_kernel(
                     out=A[:, cs], in0=A[:, cs], scalar=0.0, in1=x_sb[:, cs], op0=ALU.max, op1=ALU.mult
                 )
 
-        def b_bias(src, cs):
-            nc.vector.tensor_tensor(out=S[:, cs], in0=src, in1=bx_bc[:, cs], op=ALU.add)
+        def phase_b(pieces, stores):
+            def gate(cs):
+                nc.vector.scalar_tensor_tensor(
+                    out=S[:, cs], in0=S[:, cs], scalar=1.0, in1=A[:, cs], op0=ALU.add, op1=ALU.mult
+                )
 
-        def b_tanh(cs):
-            nc.scalar.activation(out=S[:, cs], in_=S[:, cs], func=ACT.Tanh, scale=0.5)
+            def total(cs):
+                nc.vector.tensor_tensor(out=B[:, cs], in0=B[:, cs], in1=S[:, cs], op=ALU.add)
+                if stores is None:
+                    nc.sync.dma_start(out=out[:, cs], in_=B[:, cs])
 
-        def b_gate(cs):
-            nc.vector.scalar_tensor_tensor(
-                out=S[:, cs], in0=S[:, cs], scalar=1.0, in1=A[:, cs], op0=ALU.add, op1=ALU.mult
-            )
-
-        def b_total(cs):
-            nc.vector.tensor_tensor(out=B[:, cs], in0=B[:, cs], in1=S[:, cs], op=ALU.add)
-
-        def store(cs):
-            nc.sync.dma_start(out=out[:, cs], in_=B[:, cs])
+            for src, cs in pieces:
+                nc.vector.tensor_tensor(out=S[:, cs], in0=src, in1=bx_bc[:, cs], op=ALU.add)
+            for src, cs in pieces:
+                nc.scalar.activation(out=S[:, cs], in_=S[:, cs], func=ACT.Tanh, scale=0.5)
+            gate(pieces[0][1])
+            for i in range(1, len(pieces)):
+                gate(pieces[i][1])
+                total(pieces[i - 1][1])
+            total(pieces[-1][1])
+            if stores is not None:
+                nc.sync.dma_start(out=out[:, stores], in_=B[:, stores])
 
         for jb in range(3):
             spread_softplus(jb)
@@ -247,8 +262,8 @@ def tile_cell_w_kernel(
         for jb in range(3, 6):
             spread_softplus(jb)
         mx_passes(True, wa1, 0, acc_a1, range(4, 6))
-        wx2 = [load_words(Wx_words, g, 1536, 2560, "ws%d" % g, "wx2_%d" % g) for g in range(G)]
-        wx3 = [load_words(Wx_words, g, 2560, 3072, "wt%d" % g, "wx3_%d" % g) for g in range(G)]
+        wx2 = load_range(Wx_words, 1536, 2560, "s0", "wx2")
+        wx3 = load_range(Wx_words, 2560, 3072, "s3", "wx3")
         phase_a(0, acc_a1)
         spread_bias(6, bx_bc, "bx_ps")
         acc_a2 = mx_banks(3, "a2_")
@@ -257,44 +272,18 @@ def tile_cell_w_kernel(
 
         acc_b1 = mx_banks(3, "b1_")
         mx_passes(False, wx1, 0, acc_b1, range(G))
-        c1 = [slice(NB * b, NB * (b + 1)) for b in range(3)]
-        for b in range(3):
-            b_bias(acc_b1[b][:], c1[b])
-        for b in range(3):
-            b_tanh(c1[b])
-        for b in range(3):
-            b_gate(c1[b])
-        for b in range(3):
-            b_total(c1[b])
-        store(slice(0, 1536))
-
+        phase_b(
+            [(acc_b1[b][:], slice(NB * b, NB * (b + 1))) for b in range(3)], slice(0, 1536)
+        )
         acc_b2 = mx_banks(2, "b2_")
         mx_passes(False, wx2, 1536, acc_b2, range(G))
-        c2 = [slice(1536, 1792), slice(1792, 2048), slice(2048, 2560)]
-        b_bias(acc_b2[0][:, 0:256], c2[0])
-        b_bias(acc_b2[0][:, 256:512], c2[1])
-        b_bias(acc_b2[1][:], c2[2])
-        for cs in c2:
-            b_tanh(cs)
-        b_gate(c2[0])
-        b_gate(c2[1])
-        b_total(c2[0])
-        b_total(c2[1])
-        store(slice(1536, 2048))
-        b_gate(c2[2])
-
+        phase_b(
+            [(acc_b2[b][:], slice(1536 + NB * b, 1536 + NB * (b + 1))) for b in range(2)],
+            slice(1536, 2560),
+        )
         acc_b3 = mx_banks(1, "b3_")
         mx_passes(False, wx3, 2560, acc_b3, range(G))
-        c3 = [slice(2560, 2816), slice(2816, 3072)]
-        b_bias(acc_b3[0][:, 0:256], c3[0])
-        b_bias(acc_b3[0][:, 256:512], c3[1])
-        b_tanh(c3[0])
-        b_tanh(c3[1])
-        b_total(c2[2])
-        store(c2[2])
-        b_gate(c3[0])
-        b_gate(c3[1])
-        b_total(c3[0])
-        store(c3[0])
-        b_total(c3[1])
-        store(c3[1])
+        phase_b(
+            [(acc_b3[0][:, 256 * i : 256 * (i + 1)], slice(2560 + 256 * i, 2560 + 256 * (i + 1))) for i in range(2)],
+            None,
+        )

@@ -18,7 +18,6 @@ P = 128
 D = 3072
 G = 6
 NB = 512
-GROUPS_PER_DMA = (3, 2, 1)
 
 
 def tile_cell_w_kernel(
@@ -36,7 +35,7 @@ def tile_cell_w_kernel(
         grouped = keep.tile([P, D], BF16, name="grouped", align_bytes=64)
         xcodes = keep.tile([P, G * P], U32, name="xcodes", align_bytes=64)
         xsc = keep.tile([P, G * P], U8, name="xsc", align_bytes=64)
-        planes = keep.tile([P, 3, D], U8, name="planes", align_bytes=64)
+        planes = keep.tile([P, 4, D], U8, name="planes", align_bytes=64)
         ident_f = keep.tile([P, P], F32, name="ident_f")
         ident_b = keep.tile([P, P], BF16, name="ident_b")
         zrows = keep.tile([P, NB], BF16, name="zrows")
@@ -55,19 +54,11 @@ def tile_cell_w_kernel(
         def bank(shape, dtype, name):
             return psum.tile(shape, dtype, tag="bank", name=name)
 
-        def load_range(words, c0, c1, slot, name):
-            views = []
-            g0 = 0
-            for i, n_g in enumerate(GROUPS_PER_DMA):
-                t = wpool.tile(
-                    [P, n_g, c1 - c0], U32, tag="%s_%d" % (slot, i), name="%s_%d" % (name, i), align_bytes=64
-                )
-                src = words[g0 : g0 + n_g].rearrange("g p n t -> p g (n t)")[:, :, 4 * c0 : 4 * c1]
-                nc.sync.dma_start(out=t[:].bitcast(I32), in_=src.bitcast(I32))
-                for j in range(n_g):
-                    views.append(t[:, j, :])
-                g0 += n_g
-            return views
+        def load_words(words, g, c0, c1, slot, name):
+            t = wpool.tile([P, c1 - c0], U32, tag=slot, name=name, align_bytes=64)
+            src = words[g].rearrange("p n t -> p (n t)")[:, 4 * c0 : 4 * c1]
+            nc.sync.dma_start(out=t[:].bitcast(I32), in_=src.bitcast(I32))
+            return t
 
         def table(func):
             nc.scalar.activation(out=warm2[:], in_=warm[:], func=func)
@@ -80,6 +71,7 @@ def tile_cell_w_kernel(
         nc.vector.memset(zrows[:], 0.0)
         nc.vector.memset(warm[:], 1.0)
         nc.vector.memset(planes[:, 1, :].bitcast(I32), 0)
+        nc.vector.memset(planes[:, 3, :].bitcast(I32), 0)
         nc.vector.memset(planes[:, 2, :].bitcast(I32), 0)
         nc.scalar.dma_start(out=lrows[0:24, :], in_=Lambda.rearrange("o (r c) -> (o r) c", c=P))
         nc.scalar.dma_start(out=zrows[0:6, :], in_=ba.rearrange("o (r c) -> (o r) c", c=NB))
@@ -91,7 +83,7 @@ def tile_cell_w_kernel(
         plane_loads = [
             (0, 0, 16, Wa_scales, 0, 4),
             (1, 0, 8, Wa_scales, 4, 6),
-            (1, 8, 8, Wx_scales, 4, 6),
+            (3, 8, 8, Wx_scales, 4, 6),
             (2, 0, 16, Wx_scales, 0, 4),
         ]
         for T, p0, n_p, src, g0, g1 in plane_loads:
@@ -103,12 +95,12 @@ def tile_cell_w_kernel(
         def plane_of(is_a, g):
             if g < 4:
                 return (0 if is_a else 2), 4 * g
-            return 1, (0 if is_a else 8) + 4 * (g - 4)
+            return (1 if is_a else 3), (0 if is_a else 8) + 4 * (g - 4)
 
-        wa1 = load_range(Wa_words, 0, 1536, "s0", "wa1")
+        wa1 = [load_words(Wa_words, g, 0, 1536, "ws%d" % g, "wa1_%d" % g) for g in range(G)]
         nc.sync.dma_start(out=h_sb[:], in_=ht_minus_1)
-        wa2 = load_range(Wa_words, 1536, 3072, "s1", "wa2")
-        wx1 = load_range(Wx_words, 0, 1536, "s2", "wx1")
+        wa2 = [load_words(Wa_words, g, 1536, 3072, "ws%d" % (6 + g), "wa2_%d" % g) for g in range(G)]
+        wx1 = [load_words(Wx_words, g, 0, 1536, "ws%d" % (12 + g), "wx1_%d" % g) for g in range(G)]
 
         lt_ps = bank([P, P], BF16, "lt_ps")
         nc.tensor.transpose(out=lt_ps[:], in_=lrows[:], identity=ident_b[:])
@@ -231,28 +223,22 @@ def tile_cell_w_kernel(
                     out=A[:, cs], in0=A[:, cs], scalar=0.0, in1=x_sb[:, cs], op0=ALU.max, op1=ALU.mult
                 )
 
-        def phase_b(pieces, stores):
-            def gate(cs):
-                nc.vector.scalar_tensor_tensor(
-                    out=S[:, cs], in0=S[:, cs], scalar=1.0, in1=A[:, cs], op0=ALU.add, op1=ALU.mult
-                )
+        def b_bias(src, cs):
+            nc.vector.tensor_tensor(out=S[:, cs], in0=src, in1=bx_bc[:, cs], op=ALU.add)
 
-            def total(cs):
-                nc.vector.tensor_tensor(out=B[:, cs], in0=B[:, cs], in1=S[:, cs], op=ALU.add)
-                if stores is None:
-                    nc.sync.dma_start(out=out[:, cs], in_=B[:, cs])
+        def b_tanh(cs):
+            nc.scalar.activation(out=S[:, cs], in_=S[:, cs], func=ACT.Tanh, scale=0.5)
 
-            for src, cs in pieces:
-                nc.vector.tensor_tensor(out=S[:, cs], in0=src, in1=bx_bc[:, cs], op=ALU.add)
-            for src, cs in pieces:
-                nc.scalar.activation(out=S[:, cs], in_=S[:, cs], func=ACT.Tanh, scale=0.5)
-            gate(pieces[0][1])
-            for i in range(1, len(pieces)):
-                gate(pieces[i][1])
-                total(pieces[i - 1][1])
-            total(pieces[-1][1])
-            if stores is not None:
-                nc.sync.dma_start(out=out[:, stores], in_=B[:, stores])
+        def b_gate(cs):
+            nc.vector.scalar_tensor_tensor(
+                out=S[:, cs], in0=S[:, cs], scalar=1.0, in1=A[:, cs], op0=ALU.add, op1=ALU.mult
+            )
+
+        def b_total(cs):
+            nc.vector.tensor_tensor(out=B[:, cs], in0=B[:, cs], in1=S[:, cs], op=ALU.add)
+
+        def store(cs):
+            nc.sync.dma_start(out=out[:, cs], in_=B[:, cs])
 
         for jb in range(3):
             spread_softplus(jb)
@@ -262,8 +248,8 @@ def tile_cell_w_kernel(
         for jb in range(3, 6):
             spread_softplus(jb)
         mx_passes(True, wa1, 0, acc_a1, range(4, 6))
-        wx2 = load_range(Wx_words, 1536, 2560, "s0", "wx2")
-        wx3 = load_range(Wx_words, 2560, 3072, "s3", "wx3")
+        wx2 = [load_words(Wx_words, g, 1536, 2560, "ws%d" % g, "wx2_%d" % g) for g in range(G)]
+        wx3 = [load_words(Wx_words, g, 2560, 3072, "wt%d" % g, "wx3_%d" % g) for g in range(G)]
         phase_a(0, acc_a1)
         spread_bias(6, bx_bc, "bx_ps")
         acc_a2 = mx_banks(3, "a2_")
@@ -272,18 +258,44 @@ def tile_cell_w_kernel(
 
         acc_b1 = mx_banks(3, "b1_")
         mx_passes(False, wx1, 0, acc_b1, range(G))
-        phase_b(
-            [(acc_b1[b][:], slice(NB * b, NB * (b + 1))) for b in range(3)], slice(0, 1536)
-        )
+        c1 = [slice(NB * b, NB * (b + 1)) for b in range(3)]
+        for b in range(3):
+            b_bias(acc_b1[b][:], c1[b])
+        for b in range(3):
+            b_tanh(c1[b])
+        for b in range(3):
+            b_gate(c1[b])
+        for b in range(3):
+            b_total(c1[b])
+        store(slice(0, 1536))
+
         acc_b2 = mx_banks(2, "b2_")
         mx_passes(False, wx2, 1536, acc_b2, range(G))
-        phase_b(
-            [(acc_b2[b][:], slice(1536 + NB * b, 1536 + NB * (b + 1))) for b in range(2)],
-            slice(1536, 2560),
-        )
+        c2 = [slice(1536, 1792), slice(1792, 2048), slice(2048, 2560)]
+        b_bias(acc_b2[0][:, 0:256], c2[0])
+        b_bias(acc_b2[0][:, 256:512], c2[1])
+        b_bias(acc_b2[1][:], c2[2])
+        for cs in c2:
+            b_tanh(cs)
+        b_gate(c2[0])
+        b_gate(c2[1])
+        b_total(c2[0])
+        b_total(c2[1])
+        store(slice(1536, 2048))
+        b_gate(c2[2])
+
         acc_b3 = mx_banks(1, "b3_")
         mx_passes(False, wx3, 2560, acc_b3, range(G))
-        phase_b(
-            [(acc_b3[0][:, 256 * i : 256 * (i + 1)], slice(2560 + 256 * i, 2560 + 256 * (i + 1))) for i in range(2)],
-            None,
-        )
+        c3 = [slice(2560, 2816), slice(2816, 3072)]
+        b_bias(acc_b3[0][:, 0:256], c3[0])
+        b_bias(acc_b3[0][:, 256:512], c3[1])
+        b_tanh(c3[0])
+        b_tanh(c3[1])
+        b_total(c2[2])
+        store(c2[2])
+        b_gate(c3[0])
+        b_gate(c3[1])
+        b_total(c3[0])
+        store(c3[0])
+        b_total(c3[1])
+        store(c3[1])

@@ -36,6 +36,7 @@ def tile_cell_w_kernel(
         xcodes = keep.tile([P, G * P], U32, name="xcodes", align_bytes=64)
         xsc = keep.tile([P, G * P], U8, name="xsc", align_bytes=64)
         planes = keep.tile([P, 4, D], U8, name="planes", align_bytes=64)
+        junk = keep.tile([P, 2, P], U8, name="junk")
         ident_f = keep.tile([P, P], F32, name="ident_f")
         ident_b = keep.tile([P, P], BF16, name="ident_b")
         zrows = keep.tile([P, NB], BF16, name="zrows")
@@ -65,12 +66,12 @@ def tile_cell_w_kernel(
 
         nc.sync.dma_start(out=x_sb[:], in_=xt)
         nc.vector.memset(planes[:, 0, :].bitcast(I32), 0)
+        nc.vector.memset(planes[:, 1, :].bitcast(I32), 0)
         nc.vector.memset(ident_b[:], 0.0)
         nc.vector.memset(ident_f[:], 0.0)
         nc.vector.memset(lrows[:], 0.0)
         nc.vector.memset(zrows[:], 0.0)
         nc.vector.memset(warm[:], 1.0)
-        nc.vector.memset(planes[:, 1, :].bitcast(I32), 0)
         nc.vector.memset(planes[:, 3, :].bitcast(I32), 0)
         nc.vector.memset(planes[:, 2, :].bitcast(I32), 0)
         nc.scalar.dma_start(out=lrows[0:24, :], in_=Lambda.rearrange("o (r c) -> (o r) c", c=P))
@@ -80,17 +81,38 @@ def tile_cell_w_kernel(
         make_identity(nc, ident_b[:], nomemset=True)
         make_identity(nc, ident_f[:], nomemset=True)
 
-        plane_loads = [
-            (0, 0, 16, Wa_scales, 0, 4),
-            (1, 0, 8, Wa_scales, 4, 6),
-            (3, 8, 8, Wx_scales, 4, 6),
-            (2, 0, 16, Wx_scales, 0, 4),
-        ]
-        for T, p0, n_p, src, g0, g1 in plane_loads:
-            for Q in range(4):
-                dst = planes[32 * Q + p0 : 32 * Q + p0 + n_p, T, :]
-                rows = src[g0:g1, 4 * Q : 4 * Q + 4, :]
+        wa_lo = (0, 0, 16, Wa_scales, 0, 4)
+        wa_hi = (1, 0, 8, Wa_scales, 4, 6)
+        wx_hi = (3, 8, 8, Wx_scales, 4, 6)
+        wx_lo = (2, 0, 16, Wx_scales, 0, 4)
+
+        def load_planes(spec, Q, on_sync):
+            T, p0, n_p, src, g0, g1 = spec
+            dst = planes[32 * Q + p0 : 32 * Q + p0 + n_p, T, :]
+            rows = src[g0:g1, 4 * Q : 4 * Q + 4, :]
+            if on_sync:
+                nc.sync.dma_start(out=dst.bitcast(I32), in_=rows.bitcast(I32))
+            else:
                 nc.gpsimd.dma_start(out=dst.bitcast(F32), in_=rows.bitcast(F32))
+
+        def skip_engines(i, n):
+            rows = Wa_scales.rearrange("g q n -> (g q) n")[0:n, :]
+            src = rows.rearrange("r (a b) -> r a b", a=2)[:, :, 0:64]
+            nc.gpsimd.dma_start(out=junk[0:n, i, :].bitcast(F32), in_=src.bitcast(F32))
+
+        for spec in (wa_lo, wa_hi):
+            for Q in range(2):
+                load_planes(spec, Q, True)
+        skip_engines(0, 8)
+        load_planes(wa_lo, 2, False)
+        skip_engines(1, 12)
+        load_planes(wa_lo, 3, False)
+        load_planes(wa_hi, 2, False)
+        load_planes(wa_hi, 3, False)
+        for Q in range(4):
+            load_planes(wx_hi, Q, False)
+        load_planes(wx_lo, 2, False)
+        load_planes(wx_lo, 3, False)
 
         def plane_of(is_a, g):
             if g < 4:
@@ -99,6 +121,8 @@ def tile_cell_w_kernel(
 
         wa1 = [load_words(Wa_words, g, 0, 1536, "ws%d" % g, "wa1_%d" % g) for g in range(G)]
         nc.sync.dma_start(out=h_sb[:], in_=ht_minus_1)
+        load_planes(wx_lo, 0, True)
+        load_planes(wx_lo, 1, True)
         wa2 = [load_words(Wa_words, g, 1536, 3072, "ws%d" % (6 + g), "wa2_%d" % g) for g in range(G)]
         wx1 = [load_words(Wx_words, g, 0, 1536, "ws%d" % (12 + g), "wx1_%d" % g) for g in range(G)]
 

@@ -36,7 +36,7 @@ def tile_cell_w_kernel(
         xcodes = keep.tile([P, G * P], U32, name="xcodes", align_bytes=64)
         xsc = keep.tile([P, G * P], U8, name="xsc", align_bytes=64)
         planes = keep.tile([P, 4, D], U8, name="planes", align_bytes=64)
-        junk = keep.tile([P, 2, P], U8, name="junk")
+        junk = keep.tile([P, 7, P], U8, name="junk")
         ident_f = keep.tile([P, P], F32, name="ident_f")
         ident_b = keep.tile([P, P], BF16, name="ident_b")
         zrows = keep.tile([P, NB], BF16, name="zrows")
@@ -108,11 +108,18 @@ def tile_cell_w_kernel(
         skip_engines(1, 12)
         load_planes(wa_lo, 3, False)
         load_planes(wa_hi, 2, False)
+        skip_engines(2, 10)
         load_planes(wa_hi, 3, False)
-        for Q in range(4):
-            load_planes(wx_hi, Q, False)
+        load_planes(wx_hi, 2, False)
+        skip_engines(3, 12)
         load_planes(wx_lo, 2, False)
+        skip_engines(4, 12)
         load_planes(wx_lo, 3, False)
+        skip_engines(5, 6)
+        load_planes(wx_hi, 0, False)
+        load_planes(wx_hi, 1, False)
+        load_planes(wx_hi, 3, False)
+        skip_engines(6, 8)
 
         def plane_of(is_a, g):
             if g < 4:

from contextlib import ExitStack

import concourse.mybir as mybir
from concourse.masks import make_identity

FLOPS = 2 * 128 * 3072 * 3072 * 2

F32 = mybir.dt.float32
BF16 = mybir.dt.bfloat16
I32 = mybir.dt.int32
U32 = mybir.dt.uint32
U8 = mybir.dt.uint8
FP8X4 = mybir.dt.float8_e4m3fn_x4
ACT = mybir.ActivationFunctionType
ALU = mybir.AluOpType

P = 128
D = 3072
G = 6
NB = 512


def tile_cell_w_kernel(
    tc, xt, ht_minus_1, Wa_words, Wa_scales, Wx_words, Wx_scales, ba, bx, Lambda, out
):
    nc = tc.nc
    with ExitStack() as ctx:
        keep = ctx.enter_context(tc.tile_pool(name="keep", bufs=1))
        wpool = ctx.enter_context(tc.tile_pool(name="wpool", bufs=1))
        psum = ctx.enter_context(tc.psum_pool(name="psum", bufs=8))
        ctx.enter_context(tc.manual_schedule())

        x_sb = keep.tile([P, D], BF16, name="x_sb")
        h_sb = keep.tile([P, D], BF16, name="h_sb")
        grouped = keep.tile([P, D], BF16, name="grouped", align_bytes=64)
        xcodes = keep.tile([P, G * P], U32, name="xcodes", align_bytes=64)
        xsc = keep.tile([P, G * P], U8, name="xsc", align_bytes=64)
        planes = keep.tile([P, 4, D], U8, name="planes", align_bytes=64)
        junk = keep.tile([P, 7, P], U8, name="junk")
        ident_f = keep.tile([P, P], F32, name="ident_f")
        ident_b = keep.tile([P, P], BF16, name="ident_b")
        zrows = keep.tile([P, NB], BF16, name="zrows")
        lrows = keep.tile([P, P], BF16, name="lrows")
        warm = keep.tile([P, 1], F32, name="warm")
        warm2 = keep.tile([P, 1], F32, name="warm2")
        r24 = keep.tile([P, 24], F32, name="r24")
        nv24 = keep.tile([P, 24], F32, name="nv24")
        spv = keep.tile([P, 24], F32, name="spv")
        ba_bc = keep.tile([P, D], BF16, name="ba_bc")
        bx_bc = keep.tile([P, D], BF16, name="bx_bc")
        A = keep.tile([P, D], F32, name="A")
        B = keep.tile([P, D], F32, name="B")
        S = keep.tile([P, D], F32, name="S")

        def bank(shape, dtype, name):
            return psum.tile(shape, dtype, tag="bank", name=name)

        def load_words(words, g, c0, c1, slot, name):
            t = wpool.tile([P, c1 - c0], U32, tag=slot, name=name, align_bytes=64)
            src = words[g].rearrange("p n t -> p (n t)")[:, 4 * c0 : 4 * c1]
            nc.sync.dma_start(out=t[:].bitcast(I32), in_=src.bitcast(I32))
            return t

        def table(func):
            nc.scalar.activation(out=warm2[:], in_=warm[:], func=func)

        nc.sync.dma_start(out=x_sb[:], in_=xt)
        nc.vector.memset(planes[:, 0, :].bitcast(I32), 0)
        nc.vector.memset(planes[:, 1, :].bitcast(I32), 0)
        nc.vector.memset(ident_b[:], 0.0)
        nc.vector.memset(ident_f[:], 0.0)
        nc.vector.memset(lrows[:], 0.0)
        nc.vector.memset(zrows[:], 0.0)
        nc.vector.memset(warm[:], 1.0)
        nc.vector.memset(planes[:, 3, :].bitcast(I32), 0)
        nc.vector.memset(planes[:, 2, :].bitcast(I32), 0)
        nc.scalar.dma_start(out=lrows[0:24, :], in_=Lambda.rearrange("o (r c) -> (o r) c", c=P))
        nc.scalar.dma_start(out=zrows[0:6, :], in_=ba.rearrange("o (r c) -> (o r) c", c=NB))
        nc.scalar.dma_start(out=zrows[6:12, :], in_=bx.rearrange("o (r c) -> (o r) c", c=NB))
        table(ACT.Exp)
        make_identity(nc, ident_b[:], nomemset=True)
        make_identity(nc, ident_f[:], nomemset=True)

        wa_lo = (0, 0, 16, Wa_scales, 0, 4)
        wa_hi = (1, 0, 8, Wa_scales, 4, 6)
        wx_hi = (3, 8, 8, Wx_scales, 4, 6)
        wx_lo = (2, 0, 16, Wx_scales, 0, 4)

        def load_planes(spec, Q, on_sync):
            T, p0, n_p, src, g0, g1 = spec
            dst = planes[32 * Q + p0 : 32 * Q + p0 + n_p, T, :]
            rows = src[g0:g1, 4 * Q : 4 * Q + 4, :]
            if on_sync:
                nc.sync.dma_start(out=dst.bitcast(I32), in_=rows.bitcast(I32))
            else:
                nc.gpsimd.dma_start(out=dst.bitcast(F32), in_=rows.bitcast(F32))

        def skip_engines(i, n):
            rows = Wa_scales.rearrange("g q n -> (g q) n")[0:n, :]
            src = rows.rearrange("r (a b) -> r a b", a=2)[:, :, 0:64]
            nc.gpsimd.dma_start(out=junk[0:n, i, :].bitcast(F32), in_=src.bitcast(F32))

        for spec in (wa_lo, wa_hi):
            for Q in range(2):
                load_planes(spec, Q, True)
        skip_engines(0, 8)
        load_planes(wa_lo, 2, False)
        skip_engines(1, 12)
        load_planes(wa_lo, 3, False)
        load_planes(wa_hi, 2, False)
        skip_engines(2, 10)
        load_planes(wa_hi, 3, False)
        load_planes(wx_hi, 2, False)
        skip_engines(3, 12)
        load_planes(wx_lo, 2, False)
        skip_engines(4, 12)
        load_planes(wx_lo, 3, False)
        skip_engines(5, 6)
        load_planes(wx_hi, 0, False)
        load_planes(wx_hi, 1, False)
        load_planes(wx_hi, 3, False)
        skip_engines(6, 8)

        def plane_of(is_a, g):
            if g < 4:
                return (0 if is_a else 2), 4 * g
            return (1 if is_a else 3), (0 if is_a else 8) + 4 * (g - 4)

        wa1 = [load_words(Wa_words, g, 0, 1536, "ws%d" % g, "wa1_%d" % g) for g in range(G)]
        nc.sync.dma_start(out=h_sb[:], in_=ht_minus_1)
        load_planes(wx_lo, 0, True)
        load_planes(wx_lo, 1, True)
        wa2 = [load_words(Wa_words, g, 1536, 3072, "ws%d" % (6 + g), "wa2_%d" % g) for g in range(G)]
        wx1 = [load_words(Wx_words, g, 0, 1536, "ws%d" % (12 + g), "wx1_%d" % g) for g in range(G)]

        lt_ps = bank([P, P], BF16, "lt_ps")
        nc.tensor.transpose(out=lt_ps[:], in_=lrows[:], identity=ident_b[:])
        nc.vector.tensor_scalar_max(out=r24[:], in0=lt_ps[:, 0:24], scalar1=0.0)
        nc.vector.scalar_tensor_tensor(
            out=nv24[:], in0=lt_ps[:, 0:24], scalar=0.0, in1=r24[:], op0=ALU.min, op1=ALU.subtract
        )
        nc.scalar.activation(out=nv24[:], in_=nv24[:], func=ACT.Exp)
        nc.scalar.activation(out=nv24[:], in_=nv24[:], func=ACT.Ln, bias=1.0)
        nc.vector.tensor_tensor(out=spv[:], in0=r24[:], in1=nv24[:], op=ALU.add)

        def spread_bias(row0, dst, name):
            for i in range(3):
                t = bank([P, 2 * NB], BF16, "%s%d" % (name, i))
                for half in range(2):
                    r = row0 + 2 * i + half
                    nc.tensor.matmul(
                        out=t[:, NB * half : NB * (half + 1)],
                        lhsT=ident_b[:, r : r + 1].to_broadcast([P, P]),
                        rhs=zrows[:],
                        start=True,
                        stop=True,
                    )
                nc.scalar.copy(out=dst[:, 2 * NB * i : 2 * NB * (i + 1)], in_=t[:])

        def spread_softplus(jb):
            t = bank([P, 4, P], F32, "sp_ps%d" % jb)
            for i in range(4):
                j = 4 * jb + i
                nc.tensor.transpose(
                    out=t[:, i, :], in_=spv[:, j : j + 1].to_broadcast([P, P]), identity=ident_f[:]
                )
            dst = S[:, NB * jb : NB * (jb + 1)]
            if jb % 2 == 0:
                nc.vector.tensor_copy(out=dst, in_=t[:].rearrange("p i c -> p (i c)"))
            else:
                nc.scalar.copy(out=dst, in_=t[:].rearrange("p i c -> p (i c)"))

        spread_bias(0, ba_bc, "ba_ps")

        xw = x_sb[:].bitcast(F32)
        gw = grouped[:].bitcast(F32).rearrange("p (g b u) -> p g b u", g=G, b=P, u=2)
        xt_ps = []
        for j in range(3):
            t = bank([P, 4, P], F32, "xt_ps%d" % j)
            for i in range(4):
                g, u = 2 * j + i // 2, i % 2
                nc.tensor.transpose(
                    out=t[:, i, :], in_=xw[:, 256 * g + u : 256 * (g + 1) : 2], identity=ident_f[:]
                )
            xt_ps.append(t)

        def x_out(eng_copy, j):
            eng_copy(out=gw[:, 2 * j : 2 * j + 2], in_=xt_ps[j][:].rearrange("p (g u) b -> p g b u", u=2))

        def x_quant(j):
            nc.vector.quantize_mx(
                out=xcodes[:, 256 * j : 256 * (j + 1)].bitcast(FP8X4),
                scales=xsc[:, 256 * j : 256 * (j + 1)],
                in_=grouped[:, 1024 * j : 1024 * (j + 1)],
            )

        x_out(nc.vector.tensor_copy, 0)
        x_out(nc.scalar.copy, 1)
        x_out(nc.vector.tensor_copy, 2)
        x_quant(0)
        x_quant(1)
        x_quant(2)

        def mx_banks(n_banks, name):
            return [bank([P, NB], F32, "%s%d" % (name, b)) for b in range(n_banks)]

        def mx_passes(is_a, wt, c0, acc, groups):
            for g in groups:
                T, k = plane_of(is_a, g)
                for b in range(len(acc)):
                    nc.tensor.matmul_mx(
                        out=acc[b][:],
                        lhsT=xcodes[:, P * g : P * (g + 1)].bitcast(FP8X4),
                        lhsT_scale=xsc[:, P * g : P * (g + 1)],
                        rhs=wt[g][:, NB * b : NB * (b + 1)].bitcast(FP8X4),
                        rhs_scale=planes[k:P, T, c0 + NB * b : c0 + NB * (b + 1)],
                        start=(g == 0),
                        stop=(g == G - 1),
                    )

        def phase_a(c0, acc):
            cols = [slice(c0 + NB * b, c0 + NB * (b + 1)) for b in range(len(acc))]

            def square(cs):
                nc.vector.scalar_tensor_tensor(
                    out=A[:, cs], in0=B[:, cs], scalar=-0.25, in1=B[:, cs], op0=ALU.mult, op1=ALU.mult
                )

            def times_h(cs):
                nc.vector.tensor_tensor(out=B[:, cs], in0=B[:, cs], in1=h_sb[:, cs], op=ALU.mult)

            for b, cs in enumerate(cols):
                nc.vector.tensor_tensor(out=A[:, cs], in0=acc[b][:], in1=ba_bc[:, cs], op=ALU.add)
            for cs in cols:
                nc.scalar.activation(out=A[:, cs], in_=A[:, cs], func=ACT.Tanh, scale=0.5)
            for cs in cols:
                nc.vector.scalar_tensor_tensor(
                    out=A[:, cs], in0=A[:, cs], scalar=1.0, in1=S[:, cs], op0=ALU.add, op1=ALU.mult
                )
            for cs in cols:
                nc.scalar.activation(out=B[:, cs], in_=A[:, cs], func=ACT.Exp, scale=-4.0)
            table(ACT.Sqrt)
            square(cols[0])
            square(cols[1])
            times_h(cols[0])
            square(cols[2])
            times_h(cols[1])
            times_h(cols[2])
            for cs in cols:
                nc.scalar.activation(out=A[:, cs], in_=A[:, cs], func=ACT.Sqrt, bias=0.25)
            table(ACT.Tanh)
            for cs in cols:
                nc.vector.scalar_tensor_tensor(
                    out=A[:, cs], in0=A[:, cs], scalar=0.0, in1=x_sb[:, cs], op0=ALU.max, op1=ALU.mult
                )

        def b_bias(src, cs):
            nc.vector.tensor_tensor(out=S[:, cs], in0=src, in1=bx_bc[:, cs], op=ALU.add)

        def b_tanh(cs):
            nc.scalar.activation(out=S[:, cs], in_=S[:, cs], func=ACT.Tanh, scale=0.5)

        def b_gate(cs):
            nc.vector.scalar_tensor_tensor(
                out=S[:, cs], in0=S[:, cs], scalar=1.0, in1=A[:, cs], op0=ALU.add, op1=ALU.mult
            )

        def b_total(cs):
            nc.vector.tensor_tensor(out=B[:, cs], in0=B[:, cs], in1=S[:, cs], op=ALU.add)

        def store(cs):
            nc.sync.dma_start(out=out[:, cs], in_=B[:, cs])

        for jb in range(3):
            spread_softplus(jb)
        table(ACT.Tanh)
        acc_a1 = mx_banks(3, "a1_")
        mx_passes(True, wa1, 0, acc_a1, range(0, 4))
        for jb in range(3, 6):
            spread_softplus(jb)
        mx_passes(True, wa1, 0, acc_a1, range(4, 6))
        wx2 = [load_words(Wx_words, g, 1536, 2560, "ws%d" % g, "wx2_%d" % g) for g in range(G)]
        wx3 = [load_words(Wx_words, g, 2560, 3072, "wt%d" % g, "wx3_%d" % g) for g in range(G)]
        phase_a(0, acc_a1)
        spread_bias(6, bx_bc, "bx_ps")
        acc_a2 = mx_banks(3, "a2_")
        mx_passes(True, wa2, 1536, acc_a2, range(G))
        phase_a(1536, acc_a2)

        acc_b1 = mx_banks(3, "b1_")
        mx_passes(False, wx1, 0, acc_b1, range(G))
        c1 = [slice(NB * b, NB * (b + 1)) for b in range(3)]
        for b in range(3):
            b_bias(acc_b1[b][:], c1[b])
        for b in range(3):
            b_tanh(c1[b])
        for b in range(3):
            b_gate(c1[b])
        for b in range(3):
            b_total(c1[b])
        store(slice(0, 1536))

        acc_b2 = mx_banks(2, "b2_")
        mx_passes(False, wx2, 1536, acc_b2, range(G))
        c2 = [slice(1536, 1792), slice(1792, 2048), slice(2048, 2560)]
        b_bias(acc_b2[0][:, 0:256], c2[0])
        b_bias(acc_b2[0][:, 256:512], c2[1])
        b_bias(acc_b2[1][:], c2[2])
        for cs in c2:
            b_tanh(cs)
        b_gate(c2[0])
        b_gate(c2[1])
        b_total(c2[0])
        b_total(c2[1])
        store(slice(1536, 2048))
        b_gate(c2[2])

        acc_b3 = mx_banks(1, "b3_")
        mx_passes(False, wx3, 2560, acc_b3, range(G))
        c3 = [slice(2560, 2816), slice(2816, 3072)]
        b_bias(acc_b3[0][:, 0:256], c3[0])
        b_bias(acc_b3[0][:, 256:512], c3[1])
        b_tanh(c3[0])
        b_tanh(c3[1])
        b_total(c2[2])
        store(c2[2])
        b_gate(c3[0])
        b_gate(c3[1])
        b_total(c3[0])
        store(c3[0])
        b_total(c3[1])
        store(c3[1])
